import numpy as np
import ml_dtypes


def mxq(x, axis, fmt="e4m3"):
    dtype, down = {"e4m3": (ml_dtypes.float8_e4m3fn, 7), "e5m2": (ml_dtypes.float8_e5m2, 14)}[fmt]
    v = np.moveaxis(np.asarray(x, np.float32).astype(ml_dtypes.bfloat16).astype(np.float64), axis, -1)
    blocks = v.reshape(v.shape[:-1] + (-1, 32))
    amax = np.abs(blocks).max(-1, keepdims=True)
    byte = np.maximum(np.where(amax > 0, np.frexp(amax)[1] - 1 + 127, 0) - down, 1)
    scale = np.exp2(byte - 127.0)
    codes = (blocks / scale).astype(np.float32).astype(dtype).astype(np.float64)
    return np.moveaxis((codes * scale).reshape(v.shape), -1, axis)


WIDE = False


def mx_kscale(k):
    if not WIDE:
        return np.ones(k)
    levels = np.array([10, -10, 5, -5, 0])
    if k % 512:
        return np.exp2(np.random.permutation(np.resize(levels, k // 32))).repeat(32)
    a = np.empty((k // 512, 16))
    for p in range(k // 512):
        a[p, :8] = np.random.permutation(np.resize(levels, 8))
        for g in range(8):
            far = levels[np.abs(levels - a[p, g]) >= 10]
            a[p, g + 8] = far[np.random.randint(len(far))]
    return np.exp2(a.ravel()).repeat(32)


BF16 = ml_dtypes.bfloat16


def bf(x):
    return np.asarray(x, np.float32).astype(BF16)


def f64(x):
    return np.asarray(x).astype(np.float64)


B, N, D, F, C, L = 1024, 4096, 1024, 1024, 128, 28
EPS = 1e-12


def l2norm(x):
    n = np.sqrt(np.sum(x * x, axis=1, keepdims=True))
    return x / np.maximum(n, EPS)


def setup_inputs():
    s = mx_kscale(D)
    return {"features": bf(np.random.standard_normal((B, D)) * s),
            "ex_features": bf(np.random.standard_normal((N, D)) * s),
            "g_weight": bf(np.random.standard_normal((F, D)) / np.sqrt(D) / s)}


def reference(features, ex_features, g_weight):
    gq = mxq(f64(g_weight), 1, "e4m3")
    f = mxq(f64(features), 1, "e4m3") @ gq.T
    exf = mxq(f64(ex_features), 1, "e4m3") @ gq.T
    return l2norm(f), l2norm(exf)

@@ -1,0 +1,217 @@
+from contextlib import ExitStack
+
+import concourse.mybir as mybir
+from concourse.masks import make_identity
+
+F32 = mybir.dt.float32
+BF16 = mybir.dt.bfloat16
+U32 = mybir.dt.uint32
+U8 = mybir.dt.uint8
+FP8X4 = mybir.dt.float8_e4m3fn_x4
+ACT = mybir.ActivationFunctionType
+ALU = mybir.AluOpType
+
+P = 128
+PACK = 4
+K = 1024
+K_PASS = P * PACK
+PASSES = K // K_PASS
+F_OUT = 1024
+N_TILE = 512
+HALVES = F_OUT // N_TILE
+W_TILES = F_OUT // P
+PAIR = 2
+PLANES = K // 2 // P
+TILE_WORDS = PASSES * P
+X_AHEAD = 6
+EPS = 1e-12
+
+FLOPS = 2 * (1024 + 4096) * K * F_OUT
+
+
+def tile_minerva_old_pa_kernel(tc, features, ex_features, g_weight, out_0, out_1):
+    nc = tc.nc
+
+    x_pairs = []
+    out_pairs = []
+    for x, out in ((features, out_0), (ex_features, out_1)):
+        x_view = x.rearrange("(q p a) k -> q p a k", p=P, a=PAIR)
+        out_view = out.rearrange("(q p a) f -> q p a f", p=P, a=PAIR)
+        for q in range(x.shape[0] // (P * PAIR)):
+            x_pairs.append(x_view[q])
+            out_pairs.append(out_view[q])
+    n_pairs = len(x_pairs)
+    n_tiles = n_pairs * PAIR
+    w_rows = g_weight.rearrange("(j p) k -> j p k", p=P)
+
+    with ExitStack() as ctx:
+        ctx.enter_context(tc.manual_schedule())
+        const = ctx.enter_context(tc.tile_pool(name="const", bufs=1))
+        w_in = ctx.enter_context(tc.tile_pool(name="w_in", bufs=W_TILES))
+        x_in = ctx.enter_context(tc.tile_pool(name="x_in", bufs=X_AHEAD))
+        stage = ctx.enter_context(tc.tile_pool(name="stage", bufs=3))
+        small = ctx.enter_context(tc.tile_pool(name="small", bufs=4))
+        result = ctx.enter_context(tc.tile_pool(name="result", bufs=6))
+        psum_t = ctx.enter_context(tc.psum_pool(name="psum_t", bufs=2))
+        psum_y = ctx.enter_context(tc.psum_pool(name="psum_y", bufs=6))
+
+        ident = const.tile([P, P], F32, name="ident")
+        make_identity(nc, ident[:])
+        neg_half = const.tile([P, 1], F32, name="neg_half")
+        nc.gpsimd.memset(neg_half[:], -0.5)
+
+        w_grouped = const.tile([P, PASSES * F_OUT * PACK], BF16, name="w_grouped", align_bytes=64)
+        w_codes = const.tile([P, PASSES * F_OUT], U32, name="w_codes", align_bytes=64)
+        w_scales = const.tile([P, PASSES * F_OUT], U8, name="w_scales", align_bytes=64)
+
+        w_raw = {}
+        x_raw = {}
+        banks = {}
+        grouped = {}
+        codes = {}
+        scales = {}
+        y = {}
+        sumsq = {}
+        rnorm = {}
+
+        def load_w(j):
+            w_raw[j] = w_in.tile([P, K], BF16, name="w_raw")
+            nc.sync.dma_start(out=w_raw[j][:], in_=w_rows[j])
+
+        def load_pair(q):
+            x_raw[q] = x_in.tile([P, PAIR, K], BF16, name="x_raw")
+            nc.sync.dma_start(out=x_raw[q][:], in_=x_pairs[q])
+
+        def transpose_words(rows, bank):
+            words = rows.bitcast(F32)
+            for g in range(PASSES):
+                for u in range(2):
+                    nc.tensor.transpose(
+                        bank[:, 2 * g + u, :],
+                        words[:, 2 * P * g + u : 2 * P * (g + 1) : 2],
+                        ident[:],
+                    )
+
+        def by_row(bank):
+            return bank[:].rearrange("p (g u) r -> p g r u", u=2)
+
+        def prepare_weights(h):
+            dest = w_grouped[:].bitcast(F32).rearrange("p (g f u) -> p g f u", g=PASSES, u=2)
+            for j in range(h * W_TILES // HALVES, (h + 1) * W_TILES // HALVES):
+                bank = psum_y.tile([P, PLANES, P], F32, name="w_bank", tag="acc")
+                transpose_words(w_raw[j][:], bank)
+                nc.scalar.copy(out=dest[:, :, j * P : (j + 1) * P, :], in_=by_row(bank))
+                for g in range(PASSES):
+                    lo = g * F_OUT + j * P
+                    nc.vector.quantize_mx(
+                        out=w_codes[:, lo : lo + P].bitcast(FP8X4),
+                        scales=w_scales[:, lo : lo + P],
+                        in_=w_grouped[:, lo * PACK : (lo + P) * PACK],
+                    )
+
+        def transposes(q):
+            banks[q] = []
+            for a in range(PAIR):
+                bank = psum_t.tile([P, PLANES, P], F32, name="bank")
+                transpose_words(x_raw[q][:, a, :], bank)
+                banks[q].append(bank)
+
+        def regroup(q):
+            grouped[q] = stage.tile([P, PAIR * TILE_WORDS * PACK], BF16, name="grouped", align_bytes=64)
+            dest = grouped[q][:].bitcast(F32).rearrange("p (a g r u) -> p a g r u", a=PAIR, g=PASSES, u=2)
+            for a in range(PAIR):
+                if (q * PAIR + a) % 4 == 0:
+                    nc.vector.tensor_copy(out=dest[:, a], in_=by_row(banks[q][a]))
+                else:
+                    nc.scalar.copy(out=dest[:, a], in_=by_row(banks[q][a]))
+
+        def quantise(q):
+            codes[q] = stage.tile([P, PAIR * TILE_WORDS], U32, name="codes", align_bytes=64)
+            scales[q] = stage.tile([P, PAIR * TILE_WORDS], U8, name="scales", align_bytes=64)
+            nc.vector.quantize_mx(
+                out=codes[q][:].bitcast(FP8X4), scales=scales[q][:], in_=grouped[q][:]
+            )
+
+        def multiply(i):
+            q, a = divmod(i, PAIR)
+            y[i] = []
+            for h in range(HALVES):
+                acc = psum_y.tile([P, N_TILE], F32, name="acc")
+                for g in range(PASSES):
+                    rows = slice(a * TILE_WORDS + g * P, a * TILE_WORDS + (g + 1) * P)
+                    cols = slice(g * F_OUT + h * N_TILE, g * F_OUT + (h + 1) * N_TILE)
+                    nc.tensor.matmul_mx(
+                        out=acc[:],
+                        lhsT=codes[q][:, rows].bitcast(FP8X4),
+                        lhsT_scale=scales[q][:, rows],
+                        rhs=w_codes[:, cols].bitcast(FP8X4),
+                        rhs_scale=w_scales[:, cols],
+                        start=(g == 0),
+                        stop=(g == PASSES - 1),
+                    )
+                y[i].append(acc)
+
+        def norm(i):
+            sumsq[i] = small.tile([P, HALVES], F32, name="sumsq")
+            for h in range(HALVES):
+                squares = stage.tile([P, N_TILE], F32, name="squares")
+                nc.scalar.activation(
+                    out=squares[:], in_=y[i][h][:], func=ACT.Square, accum_out=sumsq[i][:, h : h + 1]
+                )
+            clamped = small.tile([P, 1], F32, name="clamped")
+            nc.gpsimd.tensor_scalar(
+                out=clamped[:],
+                in0=sumsq[i][:, 0:1],
+                scalar1=sumsq[i][:, 1:2],
+                scalar2=EPS * EPS,
+                op0=ALU.add,
+                op1=ALU.max,
+            )
+            rnorm[i] = small.tile([P, 1], F32, name="rnorm")
+            nc.gpsimd.tensor_tensor(out=rnorm[i][:], in0=clamped[:], in1=neg_half[:], op=ALU.pow)
+
+        def scale_and_store(i):
+            q, a = divmod(i, PAIR)
+            unit = result.tile([P, F_OUT], F32, name="unit")
+            for h in range(HALVES):
+                nc.vector.tensor_scalar(
+                    out=unit[:, h * N_TILE : (h + 1) * N_TILE],
+                    in0=y[i][h][:],
+                    scalar1=rnorm[i][:, 0:1],
+                    scalar2=None,
+                    op0=ALU.mult,
+                )
+            nc.sync.dma_start(out=out_pairs[q][:, a, :], in_=unit[:])
+
+        for j in range(W_TILES // HALVES):
+            load_w(j)
+        load_pair(0)
+        for j in range(W_TILES // HALVES, W_TILES):
+            load_w(j)
+        for q in range(1, X_AHEAD):
+            load_pair(q)
+
+        prepare_weights(0)
+        transposes(0)
+        regroup(0)
+        quantise(0)
+        prepare_weights(1)
+        transposes(1)
+        regroup(1)
+
+        for i in range(n_tiles):
+            q, a = divmod(i, PAIR)
+            multiply(i)
+            norm(i)
+            if a == 0:
+                if q + X_AHEAD < n_pairs:
+                    load_pair(q + X_AHEAD)
+                if q + 2 < n_pairs:
+                    transposes(q + 2)
+                if q + 1 < n_pairs:
+                    quantise(q + 1)
+            if i >= 1:
+                scale_and_store(i - 1)
+            if a == 0 and q + 2 < n_pairs:
+                regroup(q + 2)
+        scale_and_store(n_tiles - 1)

@@ -57,8 +57,9 @@ def tile_minerva_old_pa_kernel(tc, features, ex_features, g_weight, out_0, out_1
 
         ident = const.tile([P, P], F32, name="ident")
         make_identity(nc, ident[:])
-        neg_half = const.tile([P, 1], F32, name="neg_half")
-        nc.gpsimd.memset(neg_half[:], -0.5)
+        warm = const.tile([P, 1], F32, name="warm")
+        nc.vector.memset(warm[:], 1.0)
+        nc.scalar.activation(out=warm[:], in_=warm[:], func=ACT.Abs_reciprocal_sqrt)
 
         w_grouped = const.tile([P, PASSES * F_OUT * PACK], BF16, name="w_grouped", align_bytes=64)
         w_codes = const.tile([P, PASSES * F_OUT], U32, name="w_codes", align_bytes=64)
@@ -72,7 +73,9 @@ def tile_minerva_old_pa_kernel(tc, features, ex_features, g_weight, out_0, out_1
         scales = {}
         y = {}
         sumsq = {}
+        clamped = {}
         rnorm = {}
+        unit = {}
 
         def load_w(j):
             w_raw[j] = w_in.tile([P, K], BF16, name="w_raw")
@@ -151,37 +154,41 @@ def tile_minerva_old_pa_kernel(tc, features, ex_features, g_weight, out_0, out_1
                     )
                 y[i].append(acc)
 
-        def norm(i):
-            sumsq[i] = small.tile([P, HALVES], F32, name="sumsq")
-            for h in range(HALVES):
-                squares = stage.tile([P, N_TILE], F32, name="squares")
-                nc.scalar.activation(
-                    out=squares[:], in_=y[i][h][:], func=ACT.Square, accum_out=sumsq[i][:, h : h + 1]
-                )
-            clamped = small.tile([P, 1], F32, name="clamped")
+        def square(i, h):
+            if h == 0:
+                sumsq[i] = small.tile([P, HALVES], F32, name="sumsq")
+            squares = stage.tile([P, N_TILE], F32, name="squares")
+            nc.scalar.activation(
+                out=squares[:], in_=y[i][h][:], func=ACT.Square, accum_out=sumsq[i][:, h : h + 1]
+            )
+
+        def clamp(i):
+            clamped[i] = small.tile([P, 1], F32, name="clamped")
             nc.gpsimd.tensor_scalar(
-                out=clamped[:],
+                out=clamped[i][:],
                 in0=sumsq[i][:, 0:1],
                 scalar1=sumsq[i][:, 1:2],
                 scalar2=EPS * EPS,
                 op0=ALU.add,
                 op1=ALU.max,
             )
+
+        def inverse_root(i):
             rnorm[i] = small.tile([P, 1], F32, name="rnorm")
-            nc.gpsimd.tensor_tensor(out=rnorm[i][:], in0=clamped[:], in1=neg_half[:], op=ALU.pow)
+            nc.scalar.activation(out=rnorm[i][:], in_=clamped[i][:], func=ACT.Abs_reciprocal_sqrt)
+            unit[i] = result.tile([P, F_OUT], F32, name="unit")
 
         def scale_and_store(i):
             q, a = divmod(i, PAIR)
-            unit = result.tile([P, F_OUT], F32, name="unit")
             for h in range(HALVES):
                 nc.vector.tensor_scalar(
-                    out=unit[:, h * N_TILE : (h + 1) * N_TILE],
+                    out=unit[i][:, h * N_TILE : (h + 1) * N_TILE],
                     in0=y[i][h][:],
                     scalar1=rnorm[i][:, 0:1],
                     scalar2=None,
                     op0=ALU.mult,
                 )
-            nc.sync.dma_start(out=out_pairs[q][:, a, :], in_=unit[:])
+            nc.sync.dma_start(out=out_pairs[q][:, a, :], in_=unit[i][:])
 
         for j in range(W_TILES // HALVES):
             load_w(j)
@@ -202,7 +209,11 @@ def tile_minerva_old_pa_kernel(tc, features, ex_features, g_weight, out_0, out_1
         for i in range(n_tiles):
             q, a = divmod(i, PAIR)
             multiply(i)
-            norm(i)
+            square(i, 0)
+            if i >= 1:
+                inverse_root(i - 1)
+            square(i, 1)
+            clamp(i)
             if a == 0:
                 if q + X_AHEAD < n_pairs:
                     load_pair(q + X_AHEAD)
@@ -214,4 +225,5 @@ def tile_minerva_old_pa_kernel(tc, features, ex_features, g_weight, out_0, out_1
                 scale_and_store(i - 1)
             if a == 0 and q + 2 < n_pairs:
                 regroup(q + 2)
+        inverse_root(n_tiles - 1)
         scale_and_store(n_tiles - 1)

@@ -48,6 +48,7 @@ def tile_minerva_old_pa_kernel(tc, features, ex_features, g_weight, out_0, out_1
         ctx.enter_context(tc.manual_schedule())
         const = ctx.enter_context(tc.tile_pool(name="const", bufs=1))
         w_in = ctx.enter_context(tc.tile_pool(name="w_in", bufs=W_TILES))
+        w_stage = ctx.enter_context(tc.tile_pool(name="w_stage", bufs=W_TILES))
         x_in = ctx.enter_context(tc.tile_pool(name="x_in", bufs=X_AHEAD))
         stage = ctx.enter_context(tc.tile_pool(name="stage", bufs=3))
         small = ctx.enter_context(tc.tile_pool(name="small", bufs=4))
@@ -61,11 +62,11 @@ def tile_minerva_old_pa_kernel(tc, features, ex_features, g_weight, out_0, out_1
         nc.vector.memset(warm[:], 1.0)
         nc.scalar.activation(out=warm[:], in_=warm[:], func=ACT.Abs_reciprocal_sqrt)
 
-        w_grouped = const.tile([P, PASSES * F_OUT * PACK], BF16, name="w_grouped", align_bytes=64)
         w_codes = const.tile([P, PASSES * F_OUT], U32, name="w_codes", align_bytes=64)
         w_scales = const.tile([P, PASSES * F_OUT], U8, name="w_scales", align_bytes=64)
 
         w_raw = {}
+        w_grouped = {}
         x_raw = {}
         banks = {}
         grouped = {}
@@ -98,19 +99,26 @@ def tile_minerva_old_pa_kernel(tc, features, ex_features, g_weight, out_0, out_1
         def by_row(bank):
             return bank[:].rearrange("p (g u) r -> p g r u", u=2)
 
-        def prepare_weights(h):
-            dest = w_grouped[:].bitcast(F32).rearrange("p (g f u) -> p g f u", g=PASSES, u=2)
-            for j in range(h * W_TILES // HALVES, (h + 1) * W_TILES // HALVES):
-                bank = psum_y.tile([P, PLANES, P], F32, name="w_bank", tag="acc")
-                transpose_words(w_raw[j][:], bank)
-                nc.scalar.copy(out=dest[:, :, j * P : (j + 1) * P, :], in_=by_row(bank))
-                for g in range(PASSES):
-                    lo = g * F_OUT + j * P
-                    nc.vector.quantize_mx(
-                        out=w_codes[:, lo : lo + P].bitcast(FP8X4),
-                        scales=w_scales[:, lo : lo + P],
-                        in_=w_grouped[:, lo * PACK : (lo + P) * PACK],
-                    )
+        def transpose_weights(j):
+            banks[j, "w"] = psum_y.tile([P, PLANES, P], F32, name="w_bank", tag="acc")
+            transpose_words(w_raw[j][:], banks[j, "w"])
+
+        def regroup_weights(j):
+            w_grouped[j] = w_stage.tile([P, TILE_WORDS * PACK], BF16, name="w_grouped", align_bytes=64)
+            dest = w_grouped[j][:].bitcast(F32).rearrange("p (g r u) -> p g r u", g=PASSES, u=2)
+            if j % 2 == 0:
+                nc.scalar.copy(out=dest, in_=by_row(banks[j, "w"]))
+            else:
+                nc.vector.tensor_copy(out=dest, in_=by_row(banks[j, "w"]))
+
+        def quantise_weights(j):
+            for g in range(PASSES):
+                cols = slice(g * F_OUT + j * P, g * F_OUT + (j + 1) * P)
+                nc.vector.quantize_mx(
+                    out=w_codes[:, cols].bitcast(FP8X4),
+                    scales=w_scales[:, cols],
+                    in_=w_grouped[j][:, g * P * PACK : (g + 1) * P * PACK],
+                )
 
         def transposes(q):
             banks[q] = []
@@ -119,11 +127,11 @@ def tile_minerva_old_pa_kernel(tc, features, ex_features, g_weight, out_0, out_1
                 transpose_words(x_raw[q][:, a, :], bank)
                 banks[q].append(bank)
 
-        def regroup(q):
+        def regroup(q, on_vector):
             grouped[q] = stage.tile([P, PAIR * TILE_WORDS * PACK], BF16, name="grouped", align_bytes=64)
             dest = grouped[q][:].bitcast(F32).rearrange("p (a g r u) -> p a g r u", a=PAIR, g=PASSES, u=2)
             for a in range(PAIR):
-                if (q * PAIR + a) % 4 == 0:
+                if a in on_vector:
                     nc.vector.tensor_copy(out=dest[:, a], in_=by_row(banks[q][a]))
                 else:
                     nc.scalar.copy(out=dest[:, a], in_=by_row(banks[q][a]))
@@ -162,9 +170,9 @@ def tile_minerva_old_pa_kernel(tc, features, ex_features, g_weight, out_0, out_1
                 out=squares[:], in_=y[i][h][:], func=ACT.Square, accum_out=sumsq[i][:, h : h + 1]
             )
 
-        def clamp(i):
+        def clamp(i, engine):
             clamped[i] = small.tile([P, 1], F32, name="clamped")
-            nc.gpsimd.tensor_scalar(
+            engine.tensor_scalar(
                 out=clamped[i][:],
                 in0=sumsq[i][:, 0:1],
                 scalar1=sumsq[i][:, 1:2],
@@ -178,17 +186,29 @@ def tile_minerva_old_pa_kernel(tc, features, ex_features, g_weight, out_0, out_1
             nc.scalar.activation(out=rnorm[i][:], in_=clamped[i][:], func=ACT.Abs_reciprocal_sqrt)
             unit[i] = result.tile([P, F_OUT], F32, name="unit")
 
+        def scale(i, h):
+            nc.vector.tensor_scalar(
+                out=unit[i][:, h * N_TILE : (h + 1) * N_TILE],
+                in0=y[i][h][:],
+                scalar1=rnorm[i][:, 0:1],
+                scalar2=None,
+                op0=ALU.mult,
+            )
+
         def scale_and_store(i):
             q, a = divmod(i, PAIR)
             for h in range(HALVES):
-                nc.vector.tensor_scalar(
-                    out=unit[i][:, h * N_TILE : (h + 1) * N_TILE],
-                    in0=y[i][h][:],
-                    scalar1=rnorm[i][:, 0:1],
-                    scalar2=None,
-                    op0=ALU.mult,
-                )
+                scale(i, h)
             nc.sync.dma_start(out=out_pairs[q][:, a, :], in_=unit[i][:])
+
+        def scale_and_store_last(i):
+            q, a = divmod(i, PAIR)
+            nc.scalar.activation(
+                out=unit[i][:, 0:N_TILE], in_=y[i][0][:], func=ACT.Copy, scale=rnorm[i][:, 0:1]
+            )
+            scale(i, 1)
+            nc.scalar.dma_start(out=out_pairs[q][:, a, 0:N_TILE], in_=unit[i][:, 0:N_TILE])
+            nc.sync.dma_start(out=out_pairs[q][:, a, N_TILE:F_OUT], in_=unit[i][:, N_TILE:F_OUT])
 
         for j in range(W_TILES // HALVES):
             load_w(j)
@@ -198,13 +218,19 @@ def tile_minerva_old_pa_kernel(tc, features, ex_features, g_weight, out_0, out_1
         for q in range(1, X_AHEAD):
             load_pair(q)
 
-        prepare_weights(0)
-        transposes(0)
-        regroup(0)
-        quantise(0)
-        prepare_weights(1)
+        for j in range(W_TILES):
+            if j == W_TILES // HALVES:
+                transposes(0)
+                regroup(0, on_vector=(1,))
+            transpose_weights(j)
+            regroup_weights(j)
+            if j >= 1:
+                quantise_weights(j - 1)
+            if j == W_TILES // HALVES:
+                quantise(0)
+        quantise_weights(W_TILES - 1)
         transposes(1)
-        regroup(1)
+        regroup(1, on_vector=())
 
         for i in range(n_tiles):
             q, a = divmod(i, PAIR)
@@ -213,7 +239,8 @@ def tile_minerva_old_pa_kernel(tc, features, ex_features, g_weight, out_0, out_1
             if i >= 1:
                 inverse_root(i - 1)
             square(i, 1)
-            clamp(i)
+            if i < n_tiles - 1:
+                clamp(i, nc.gpsimd)
             if a == 0:
                 if q + X_AHEAD < n_pairs:
                     load_pair(q + X_AHEAD)
@@ -224,6 +251,7 @@ def tile_minerva_old_pa_kernel(tc, features, ex_features, g_weight, out_0, out_1
             if i >= 1:
                 scale_and_store(i - 1)
             if a == 0 and q + 2 < n_pairs:
-                regroup(q + 2)
+                regroup(q + 2, on_vector=(0,) if q % 2 == 0 else ())
+        clamp(n_tiles - 1, nc.vector)
         inverse_root(n_tiles - 1)
-        scale_and_store(n_tiles - 1)
+        scale_and_store_last(n_tiles - 1)

@@ -62,6 +62,8 @@ def tile_minerva_old_pa_kernel(tc, features, ex_features, g_weight, out_0, out_1
         nc.vector.memset(warm[:], 1.0)
         nc.scalar.activation(out=warm[:], in_=warm[:], func=ACT.Abs_reciprocal_sqrt)
 
+        zeros = const.tile([P, N_TILE], BF16, name="zeros")
+        nc.vector.memset(zeros[:], 0.0)
         w_codes = const.tile([P, PASSES * F_OUT], U32, name="w_codes", align_bytes=64)
         w_scales = const.tile([P, PASSES * F_OUT], U8, name="w_scales", align_bytes=64)
 
@@ -99,6 +101,11 @@ def tile_minerva_old_pa_kernel(tc, features, ex_features, g_weight, out_0, out_1
         def by_row(bank):
             return bank[:].rearrange("p (g u) r -> p g r u", u=2)
 
+        def keep_clock(n):
+            idle = psum_y.tile([P, N_TILE], F32, name="idle", tag="acc")
+            for c in range(n):
+                nc.tensor.matmul(out=idle[:], lhsT=zeros[:, 0:P], rhs=zeros[:], start=True, stop=True)
+
         def transpose_weights(j):
             banks[j, "w"] = psum_y.tile([P, PLANES, P], F32, name="w_bank", tag="acc")
             transpose_words(w_raw[j][:], banks[j, "w"])
@@ -106,7 +113,7 @@ def tile_minerva_old_pa_kernel(tc, features, ex_features, g_weight, out_0, out_1
         def regroup_weights(j):
             w_grouped[j] = w_stage.tile([P, TILE_WORDS * PACK], BF16, name="w_grouped", align_bytes=64)
             dest = w_grouped[j][:].bitcast(F32).rearrange("p (g r u) -> p g r u", g=PASSES, u=2)
-            if j % 2 == 0:
+            if j % 2 == 1:
                 nc.scalar.copy(out=dest, in_=by_row(banks[j, "w"]))
             else:
                 nc.vector.tensor_copy(out=dest, in_=by_row(banks[j, "w"]))
@@ -143,31 +150,28 @@ def tile_minerva_old_pa_kernel(tc, features, ex_features, g_weight, out_0, out_1
                 out=codes[q][:].bitcast(FP8X4), scales=scales[q][:], in_=grouped[q][:]
             )
 
-        def multiply(i):
+        def multiply(i, h):
             q, a = divmod(i, PAIR)
-            y[i] = []
-            for h in range(HALVES):
-                acc = psum_y.tile([P, N_TILE], F32, name="acc")
-                for g in range(PASSES):
-                    rows = slice(a * TILE_WORDS + g * P, a * TILE_WORDS + (g + 1) * P)
-                    cols = slice(g * F_OUT + h * N_TILE, g * F_OUT + (h + 1) * N_TILE)
-                    nc.tensor.matmul_mx(
-                        out=acc[:],
-                        lhsT=codes[q][:, rows].bitcast(FP8X4),
-                        lhsT_scale=scales[q][:, rows],
-                        rhs=w_codes[:, cols].bitcast(FP8X4),
-                        rhs_scale=w_scales[:, cols],
-                        start=(g == 0),
-                        stop=(g == PASSES - 1),
-                    )
-                y[i].append(acc)
+            y[i, h] = psum_y.tile([P, N_TILE], F32, name="acc")
+            for g in range(PASSES):
+                rows = slice(a * TILE_WORDS + g * P, a * TILE_WORDS + (g + 1) * P)
+                cols = slice(g * F_OUT + h * N_TILE, g * F_OUT + (h + 1) * N_TILE)
+                nc.tensor.matmul_mx(
+                    out=y[i, h][:],
+                    lhsT=codes[q][:, rows].bitcast(FP8X4),
+                    lhsT_scale=scales[q][:, rows],
+                    rhs=w_codes[:, cols].bitcast(FP8X4),
+                    rhs_scale=w_scales[:, cols],
+                    start=(g == 0),
+                    stop=(g == PASSES - 1),
+                )
 
         def square(i, h):
             if h == 0:
                 sumsq[i] = small.tile([P, HALVES], F32, name="sumsq")
             squares = stage.tile([P, N_TILE], F32, name="squares")
             nc.scalar.activation(
-                out=squares[:], in_=y[i][h][:], func=ACT.Square, accum_out=sumsq[i][:, h : h + 1]
+                out=squares[:], in_=y[i, h][:], func=ACT.Square, accum_out=sumsq[i][:, h : h + 1]
             )
 
         def clamp(i, engine):
@@ -189,26 +193,29 @@ def tile_minerva_old_pa_kernel(tc, features, ex_features, g_weight, out_0, out_1
         def scale(i, h):
             nc.vector.tensor_scalar(
                 out=unit[i][:, h * N_TILE : (h + 1) * N_TILE],
-                in0=y[i][h][:],
+                in0=y[i, h][:],
                 scalar1=rnorm[i][:, 0:1],
                 scalar2=None,
                 op0=ALU.mult,
             )
 
-        def scale_and_store(i):
+        def scale_on_scalar(i, h):
+            nc.scalar.activation(
+                out=unit[i][:, h * N_TILE : (h + 1) * N_TILE],
+                in_=y[i, h][:],
+                func=ACT.Copy,
+                scale=rnorm[i][:, 0:1],
+            )
+
+        def store(i):
             q, a = divmod(i, PAIR)
-            for h in range(HALVES):
-                scale(i, h)
             nc.sync.dma_start(out=out_pairs[q][:, a, :], in_=unit[i][:])
 
-        def scale_and_store_last(i):
+        def store_halves(i):
             q, a = divmod(i, PAIR)
-            nc.scalar.activation(
-                out=unit[i][:, 0:N_TILE], in_=y[i][0][:], func=ACT.Copy, scale=rnorm[i][:, 0:1]
-            )
-            scale(i, 1)
-            nc.scalar.dma_start(out=out_pairs[q][:, a, 0:N_TILE], in_=unit[i][:, 0:N_TILE])
-            nc.sync.dma_start(out=out_pairs[q][:, a, N_TILE:F_OUT], in_=unit[i][:, N_TILE:F_OUT])
+            for engine, h in ((nc.scalar, 0), (nc.sync, 1)):
+                cols = slice(h * N_TILE, (h + 1) * N_TILE)
+                engine.dma_start(out=out_pairs[q][:, a, cols], in_=unit[i][:, cols])
 
         for j in range(W_TILES // HALVES):
             load_w(j)
@@ -218,9 +225,13 @@ def tile_minerva_old_pa_kernel(tc, features, ex_features, g_weight, out_0, out_1
         for q in range(1, X_AHEAD):
             load_pair(q)
 
+        keep_clock(5)
         for j in range(W_TILES):
+            if j in (2, 4, 6):
+                keep_clock(1)
             if j == W_TILES // HALVES:
                 transposes(0)
+                keep_clock(1)
                 regroup(0, on_vector=(1,))
             transpose_weights(j)
             regroup_weights(j)
@@ -228,19 +239,28 @@ def tile_minerva_old_pa_kernel(tc, features, ex_features, g_weight, out_0, out_1
                 quantise_weights(j - 1)
             if j == W_TILES // HALVES:
                 quantise(0)
+        for a in range(PAIR):
+            multiply(a, 0)
+            square(a, 0)
         quantise_weights(W_TILES - 1)
         transposes(1)
-        regroup(1, on_vector=())
+        regroup(1, on_vector=(0, 1))
+        for a in range(PAIR):
+            multiply(a, 1)
+            square(a, 1)
+            clamp(a, nc.gpsimd)
+        inverse_root(0)
 
         for i in range(n_tiles):
             q, a = divmod(i, PAIR)
-            multiply(i)
-            square(i, 0)
-            if i >= 1:
+            if q >= 1:
+                multiply(i, 0)
+                multiply(i, 1)
+                square(i, 0)
                 inverse_root(i - 1)
-            square(i, 1)
-            if i < n_tiles - 1:
-                clamp(i, nc.gpsimd)
+                square(i, 1)
+                if i < n_tiles - 1:
+                    clamp(i, nc.gpsimd)
             if a == 0:
                 if q + X_AHEAD < n_pairs:
                     load_pair(q + X_AHEAD)
@@ -248,10 +268,19 @@ def tile_minerva_old_pa_kernel(tc, features, ex_features, g_weight, out_0, out_1
                     transposes(q + 2)
                 if q + 1 < n_pairs:
                     quantise(q + 1)
-            if i >= 1:
-                scale_and_store(i - 1)
+            if 1 <= i < n_tiles - 1:
+                scale(i - 1, 0)
+                scale(i - 1, 1)
+                store(i - 1)
             if a == 0 and q + 2 < n_pairs:
                 regroup(q + 2, on_vector=(0,) if q % 2 == 0 else ())
-        clamp(n_tiles - 1, nc.vector)
-        inverse_root(n_tiles - 1)
-        scale_and_store_last(n_tiles - 1)
+
+        last = n_tiles - 1
+        scale(last - 1, 1)
+        scale_on_scalar(last - 1, 0)
+        store(last - 1)
+        clamp(last, nc.vector)
+        inverse_root(last)
+        scale_on_scalar(last, 0)
+        scale(last, 1)
+        store_halves(last)

@@ -24,6 +24,7 @@ PAIR = 2
 PLANES = K // 2 // P
 TILE_WORDS = PASSES * P
 X_AHEAD = 6
+BY_HALVES = 4
 EPS = 1e-12
 
 FLOPS = 2 * (1024 + 4096) * K * F_OUT
@@ -84,6 +85,11 @@ def tile_minerva_old_pa_kernel(tc, features, ex_features, g_weight, out_0, out_1
             w_raw[j] = w_in.tile([P, K], BF16, name="w_raw")
             nc.sync.dma_start(out=w_raw[j][:], in_=w_rows[j])
 
+        def load_first_pair(a):
+            if a == 0:
+                x_raw[0] = x_in.tile([P, PAIR, K], BF16, name="x_raw")
+            nc.sync.dma_start(out=x_raw[0][:, a, :], in_=x_pairs[0][:, a, :])
+
         def load_pair(q):
             x_raw[q] = x_in.tile([P, PAIR, K], BF16, name="x_raw")
             nc.sync.dma_start(out=x_raw[q][:], in_=x_pairs[q])
@@ -127,27 +133,36 @@ def tile_minerva_old_pa_kernel(tc, features, ex_features, g_weight, out_0, out_1
                     in_=w_grouped[j][:, g * P * PACK : (g + 1) * P * PACK],
                 )
 
-        def transposes(q):
-            banks[q] = []
-            for a in range(PAIR):
-                bank = psum_t.tile([P, PLANES, P], F32, name="bank")
-                transpose_words(x_raw[q][:, a, :], bank)
-                banks[q].append(bank)
+        def transposes(q, tiles=range(PAIR)):
+            for a in tiles:
+                banks[q, a] = psum_t.tile([P, PLANES, P], F32, name="bank")
+                transpose_words(x_raw[q][:, a, :], banks[q, a])
 
-        def regroup(q, on_vector):
-            grouped[q] = stage.tile([P, PAIR * TILE_WORDS * PACK], BF16, name="grouped", align_bytes=64)
+        def copy_planes(q, a, passes, copy):
             dest = grouped[q][:].bitcast(F32).rearrange("p (a g r u) -> p a g r u", a=PAIR, g=PASSES, u=2)
-            for a in range(PAIR):
-                if a in on_vector:
-                    nc.vector.tensor_copy(out=dest[:, a], in_=by_row(banks[q][a]))
-                else:
-                    nc.scalar.copy(out=dest[:, a], in_=by_row(banks[q][a]))
+            copy(out=dest[:, a, passes], in_=by_row(banks[q, a])[:, passes])
 
-        def quantise(q):
-            codes[q] = stage.tile([P, PAIR * TILE_WORDS], U32, name="codes", align_bytes=64)
-            scales[q] = stage.tile([P, PAIR * TILE_WORDS], U8, name="scales", align_bytes=64)
+        def regroup(q, on_vector, tiles=range(PAIR)):
+            if q not in grouped:
+                grouped[q] = stage.tile([P, PAIR * TILE_WORDS * PACK], BF16, name="grouped", align_bytes=64)
+            for a in tiles:
+                copy_planes(q, a, slice(0, PASSES), nc.vector.tensor_copy if a in on_vector else nc.scalar.copy)
+
+        def regroup_shared(q):
+            regroup(q, (), ())
+            copy_planes(q, 0, slice(1, 2), nc.scalar.copy)
+            copy_planes(q, 1, slice(0, PASSES), nc.scalar.copy)
+            copy_planes(q, 0, slice(0, 1), nc.vector.tensor_copy)
+
+        def quantise(q, tiles=range(PAIR)):
+            if 0 in tiles:
+                codes[q] = stage.tile([P, PAIR * TILE_WORDS], U32, name="codes", align_bytes=64)
+                scales[q] = stage.tile([P, PAIR * TILE_WORDS], U8, name="scales", align_bytes=64)
+            words = slice(tiles[0] * TILE_WORDS, (tiles[-1] + 1) * TILE_WORDS)
             nc.vector.quantize_mx(
-                out=codes[q][:].bitcast(FP8X4), scales=scales[q][:], in_=grouped[q][:]
+                out=codes[q][:, words].bitcast(FP8X4),
+                scales=scales[q][:, words],
+                in_=grouped[q][:, words.start * PACK : words.stop * PACK],
             )
 
         def multiply(i, h):
@@ -211,44 +226,49 @@ def tile_minerva_old_pa_kernel(tc, features, ex_features, g_weight, out_0, out_1
             q, a = divmod(i, PAIR)
             nc.sync.dma_start(out=out_pairs[q][:, a, :], in_=unit[i][:])
 
-        def store_halves(i):
+        def store_half(i, h, engine):
             q, a = divmod(i, PAIR)
-            for engine, h in ((nc.scalar, 0), (nc.sync, 1)):
-                cols = slice(h * N_TILE, (h + 1) * N_TILE)
-                engine.dma_start(out=out_pairs[q][:, a, cols], in_=unit[i][:, cols])
+            cols = slice(h * N_TILE, (h + 1) * N_TILE)
+            engine.dma_start(out=out_pairs[q][:, a, cols], in_=unit[i][:, cols])
 
         for j in range(W_TILES // HALVES):
             load_w(j)
-        load_pair(0)
+        load_first_pair(0)
         for j in range(W_TILES // HALVES, W_TILES):
             load_w(j)
+        load_first_pair(1)
         for q in range(1, X_AHEAD):
             load_pair(q)
 
-        keep_clock(5)
+        first, second = (0,), (1,)
+        keep_clock(3)
         for j in range(W_TILES):
             if j in (2, 4, 6):
                 keep_clock(1)
             if j == W_TILES // HALVES:
-                transposes(0)
-                keep_clock(1)
-                regroup(0, on_vector=(1,))
+                transposes(0, first)
+                regroup(0, (), first)
             transpose_weights(j)
             regroup_weights(j)
             if j >= 1:
                 quantise_weights(j - 1)
             if j == W_TILES // HALVES:
-                quantise(0)
-        for a in range(PAIR):
-            multiply(a, 0)
-            square(a, 0)
+                quantise(0, first)
+        transposes(0, second)
+        regroup(0, (), second)
+        multiply(0, 0)
+        square(0, 0)
         quantise_weights(W_TILES - 1)
+        quantise(0, second)
         transposes(1)
         regroup(1, on_vector=(0, 1))
-        for a in range(PAIR):
-            multiply(a, 1)
-            square(a, 1)
-            clamp(a, nc.gpsimd)
+        multiply(0, 1)
+        square(0, 1)
+        clamp(0, nc.gpsimd)
+        for h in range(HALVES):
+            multiply(1, h)
+            square(1, h)
+        clamp(1, nc.gpsimd)
         inverse_root(0)
 
         for i in range(n_tiles):
@@ -269,18 +289,25 @@ def tile_minerva_old_pa_kernel(tc, features, ex_features, g_weight, out_0, out_1
                 if q + 1 < n_pairs:
                     quantise(q + 1)
             if 1 <= i < n_tiles - 1:
-                scale(i - 1, 0)
-                scale(i - 1, 1)
-                store(i - 1)
+                if i - 1 < n_tiles - BY_HALVES:
+                    scale(i - 1, 0)
+                    scale(i - 1, 1)
+                    store(i - 1)
+                else:
+                    for h in range(HALVES):
+                        scale(i - 1, h)
+                        store_half(i - 1, h, nc.sync)
             if a == 0 and q + 2 < n_pairs:
-                regroup(q + 2, on_vector=(0,) if q % 2 == 0 else ())
+                regroup_shared(q + 2)
 
         last = n_tiles - 1
         scale(last - 1, 1)
+        store_half(last - 1, 1, nc.sync)
         scale_on_scalar(last - 1, 0)
-        store(last - 1)
+        store_half(last - 1, 0, nc.sync)
         clamp(last, nc.vector)
         inverse_root(last)
         scale_on_scalar(last, 0)
+        store_half(last, 0, nc.scalar)
         scale(last, 1)
-        store_halves(last)
+        store_half(last, 1, nc.sync)

@@ -51,6 +51,7 @@ def tile_minerva_old_pa_kernel(tc, features, ex_features, g_weight, out_0, out_1
         w_in = ctx.enter_context(tc.tile_pool(name="w_in", bufs=W_TILES))
         w_stage = ctx.enter_context(tc.tile_pool(name="w_stage", bufs=W_TILES))
         x_in = ctx.enter_context(tc.tile_pool(name="x_in", bufs=X_AHEAD))
+        parted = ctx.enter_context(tc.tile_pool(name="parted", bufs=3))
         stage = ctx.enter_context(tc.tile_pool(name="stage", bufs=3))
         small = ctx.enter_context(tc.tile_pool(name="small", bufs=4))
         result = ctx.enter_context(tc.tile_pool(name="result", bufs=6))
@@ -71,6 +72,7 @@ def tile_minerva_old_pa_kernel(tc, features, ex_features, g_weight, out_0, out_1
         w_raw = {}
         w_grouped = {}
         x_raw = {}
+        even_odd = {}
         banks = {}
         grouped = {}
         codes = {}
@@ -94,15 +96,21 @@ def tile_minerva_old_pa_kernel(tc, features, ex_features, g_weight, out_0, out_1
             x_raw[q] = x_in.tile([P, PAIR, K], BF16, name="x_raw")
             nc.sync.dma_start(out=x_raw[q][:], in_=x_pairs[q])
 
-        def transpose_words(rows, bank):
+        def transpose_words(rows, bank, parted_pass=None):
             words = rows.bitcast(F32)
             for g in range(PASSES):
                 for u in range(2):
-                    nc.tensor.transpose(
-                        bank[:, 2 * g + u, :],
-                        words[:, 2 * P * g + u : 2 * P * (g + 1) : 2],
-                        ident[:],
-                    )
+                    every_2nd = words[:, 2 * P * g + u : 2 * P * (g + 1) : 2]
+                    if g == 0 and parted_pass is not None:
+                        every_2nd = parted_pass[:, u, :]
+                    nc.tensor.transpose(bank[:, 2 * g + u, :], every_2nd, ident[:])
+
+        def part_even_odd(q):
+            even_odd[q, 0] = parted.tile([P, 2, P], F32, name="even_odd")
+            nc.vector.tensor_copy(
+                out=even_odd[q, 0][:],
+                in_=x_raw[q][:, 0, 0:K_PASS].bitcast(F32).rearrange("p (w u) -> p u w", u=2),
+            )
 
         def by_row(bank):
             return bank[:].rearrange("p (g u) r -> p g r u", u=2)
@@ -136,7 +144,7 @@ def tile_minerva_old_pa_kernel(tc, features, ex_features, g_weight, out_0, out_1
         def transposes(q, tiles=range(PAIR)):
             for a in tiles:
                 banks[q, a] = psum_t.tile([P, PLANES, P], F32, name="bank")
-                transpose_words(x_raw[q][:, a, :], banks[q, a])
+                transpose_words(x_raw[q][:, a, :], banks[q, a], even_odd.get((q, a)))
 
         def copy_planes(q, a, passes, copy):
             dest = grouped[q][:].bitcast(F32).rearrange("p (a g r u) -> p a g r u", a=PAIR, g=PASSES, u=2)
@@ -241,7 +249,7 @@ def tile_minerva_old_pa_kernel(tc, features, ex_features, g_weight, out_0, out_1
             load_pair(q)
 
         first, second = (0,), (1,)
-        keep_clock(3)
+        keep_clock(5)
         for j in range(W_TILES):
             if j in (2, 4, 6):
                 keep_clock(1)
@@ -288,6 +296,8 @@ def tile_minerva_old_pa_kernel(tc, features, ex_features, g_weight, out_0, out_1
                     transposes(q + 2)
                 if q + 1 < n_pairs:
                     quantise(q + 1)
+            if a == 1 and q + 3 < n_pairs:
+                part_even_odd(q + 3)
             if 1 <= i < n_tiles - 1:
                 if i - 1 < n_tiles - BY_HALVES:
                     scale(i - 1, 0)

@@ -287,8 +287,6 @@ def tile_minerva_old_pa_kernel(tc, features, ex_features, g_weight, out_0, out_1
                 square(i, 0)
                 inverse_root(i - 1)
                 square(i, 1)
-                if i < n_tiles - 1:
-                    clamp(i, nc.gpsimd)
             if a == 0:
                 if q + X_AHEAD < n_pairs:
                     load_pair(q + X_AHEAD)
@@ -299,14 +297,16 @@ def tile_minerva_old_pa_kernel(tc, features, ex_features, g_weight, out_0, out_1
             if a == 1 and q + 3 < n_pairs:
                 part_even_odd(q + 3)
             if 1 <= i < n_tiles - 1:
+                scale(i - 1, 0)
+                if i - 1 >= n_tiles - BY_HALVES:
+                    store_half(i - 1, 0, nc.sync)
+                if q >= 1:
+                    clamp(i, nc.vector)
+                scale(i - 1, 1)
                 if i - 1 < n_tiles - BY_HALVES:
-                    scale(i - 1, 0)
-                    scale(i - 1, 1)
                     store(i - 1)
                 else:
-                    for h in range(HALVES):
-                        scale(i - 1, h)
-                        store_half(i - 1, h, nc.sync)
+                    store_half(i - 1, 1, nc.sync)
             if a == 0 and q + 2 < n_pairs:
                 regroup_shared(q + 2)
 

@@ -96,21 +96,26 @@ def tile_minerva_old_pa_kernel(tc, features, ex_features, g_weight, out_0, out_1
             x_raw[q] = x_in.tile([P, PAIR, K], BF16, name="x_raw")
             nc.sync.dma_start(out=x_raw[q][:], in_=x_pairs[q])
 
-        def transpose_words(rows, bank, parted_pass=None):
+        def transpose_words(rows, bank, parted_words=None):
             words = rows.bitcast(F32)
             for g in range(PASSES):
                 for u in range(2):
                     every_2nd = words[:, 2 * P * g + u : 2 * P * (g + 1) : 2]
-                    if g == 0 and parted_pass is not None:
-                        every_2nd = parted_pass[:, u, :]
+                    if parted_words is not None:
+                        every_2nd = parted_words[:, g, u, :].bitcast(F32)
                     nc.tensor.transpose(bank[:, 2 * g + u, :], every_2nd, ident[:])
 
-        def part_even_odd(q):
-            even_odd[q, 0] = parted.tile([P, 2, P], F32, name="even_odd")
-            nc.vector.tensor_copy(
-                out=even_odd[q, 0][:],
-                in_=x_raw[q][:, 0, 0:K_PASS].bitcast(F32).rearrange("p (w u) -> p u w", u=2),
-            )
+        def part_even_odd(q, a):
+            even_odd[q, a] = parted.tile([P, PASSES, 2, 2 * P], BF16, name="even_odd", align_bytes=64)
+            for g in range(PASSES):
+                nc.gpsimd.tensor_scalar(
+                    out=even_odd[q, a][:, g].rearrange("p u (w e) -> p u w e", e=2),
+                    in0=x_raw[q][:, a, g * K_PASS : (g + 1) * K_PASS].rearrange("p (w u e) -> p u w e", u=2, e=2),
+                    scalar1=1.0,
+                    scalar2=0.0,
+                    op0=ALU.mult,
+                    op1=ALU.add,
+                )
 
         def by_row(bank):
             return bank[:].rearrange("p (g u) r -> p g r u", u=2)
@@ -295,7 +300,8 @@ def tile_minerva_old_pa_kernel(tc, features, ex_features, g_weight, out_0, out_1
                 if q + 1 < n_pairs:
                     quantise(q + 1)
             if a == 1 and q + 3 < n_pairs:
-                part_even_odd(q + 3)
+                for b in (0,):
+                    part_even_odd(q + 3, b)
             if 1 <= i < n_tiles - 1:
                 scale(i - 1, 0)
                 if i - 1 >= n_tiles - BY_HALVES:

@@ -23,7 +23,7 @@ W_TILES = F_OUT // P
 PAIR = 2
 PLANES = K // 2 // P
 TILE_WORDS = PASSES * P
-X_AHEAD = 6
+X_AHEAD = 8
 BY_HALVES = 4
 EPS = 1e-12
 
@@ -54,7 +54,7 @@ def tile_minerva_old_pa_kernel(tc, features, ex_features, g_weight, out_0, out_1
         parted = ctx.enter_context(tc.tile_pool(name="parted", bufs=3))
         stage = ctx.enter_context(tc.tile_pool(name="stage", bufs=3))
         small = ctx.enter_context(tc.tile_pool(name="small", bufs=4))
-        result = ctx.enter_context(tc.tile_pool(name="result", bufs=6))
+        result = ctx.enter_context(tc.tile_pool(name="result", bufs=10))
         psum_t = ctx.enter_context(tc.psum_pool(name="psum_t", bufs=2))
         psum_y = ctx.enter_context(tc.psum_pool(name="psum_y", bufs=6))
 
@@ -132,7 +132,7 @@ def tile_minerva_old_pa_kernel(tc, features, ex_features, g_weight, out_0, out_1
         def regroup_weights(j):
             w_grouped[j] = w_stage.tile([P, TILE_WORDS * PACK], BF16, name="w_grouped", align_bytes=64)
             dest = w_grouped[j][:].bitcast(F32).rearrange("p (g r u) -> p g r u", g=PASSES, u=2)
-            if j % 2 == 1:
+            if j % 3 != 0:
                 nc.scalar.copy(out=dest, in_=by_row(banks[j, "w"]))
             else:
                 nc.vector.tensor_copy(out=dest, in_=by_row(banks[j, "w"]))
@@ -277,12 +277,17 @@ def tile_minerva_old_pa_kernel(tc, features, ex_features, g_weight, out_0, out_1
         regroup(1, on_vector=(0, 1))
         multiply(0, 1)
         square(0, 1)
-        clamp(0, nc.gpsimd)
-        for h in range(HALVES):
-            multiply(1, h)
-            square(1, h)
-        clamp(1, nc.gpsimd)
+        quantise(1)
+        clamp(0, nc.vector)
+        multiply(1, 0)
+        square(1, 0)
         inverse_root(0)
+        multiply(1, 1)
+        square(1, 1)
+        scale(0, 0)
+        clamp(1, nc.vector)
+        scale(0, 1)
+        store(0)
 
         for i in range(n_tiles):
             q, a = divmod(i, PAIR)
@@ -297,12 +302,12 @@ def tile_minerva_old_pa_kernel(tc, features, ex_features, g_weight, out_0, out_1
                     load_pair(q + X_AHEAD)
                 if q + 2 < n_pairs:
                     transposes(q + 2)
-                if q + 1 < n_pairs:
+                if 1 <= q < n_pairs - 1:
                     quantise(q + 1)
             if a == 1 and q + 3 < n_pairs:
                 for b in (0,):
                     part_even_odd(q + 3, b)
-            if 1 <= i < n_tiles - 1:
+            if 2 <= i < n_tiles - 1:
                 scale(i - 1, 0)
                 if i - 1 >= n_tiles - BY_HALVES:
                     store_half(i - 1, 0, nc.sync)

@@ -151,21 +151,21 @@ def tile_minerva_old_pa_kernel(tc, features, ex_features, g_weight, out_0, out_1
                 banks[q, a] = psum_t.tile([P, PLANES, P], F32, name="bank")
                 transpose_words(x_raw[q][:, a, :], banks[q, a], even_odd.get((q, a)))
 
-        def copy_planes(q, a, passes, copy):
+        def copy_planes(q, a, rows, copy):
             dest = grouped[q][:].bitcast(F32).rearrange("p (a g r u) -> p a g r u", a=PAIR, g=PASSES, u=2)
-            copy(out=dest[:, a, passes], in_=by_row(banks[q, a])[:, passes])
+            copy(out=dest[:, a, :, rows], in_=by_row(banks[q, a])[:, :, rows])
 
         def regroup(q, on_vector, tiles=range(PAIR)):
             if q not in grouped:
                 grouped[q] = stage.tile([P, PAIR * TILE_WORDS * PACK], BF16, name="grouped", align_bytes=64)
             for a in tiles:
-                copy_planes(q, a, slice(0, PASSES), nc.vector.tensor_copy if a in on_vector else nc.scalar.copy)
+                copy_planes(q, a, slice(0, P), nc.vector.tensor_copy if a in on_vector else nc.scalar.copy)
 
         def regroup_shared(q):
             regroup(q, (), ())
-            copy_planes(q, 0, slice(1, 2), nc.scalar.copy)
-            copy_planes(q, 1, slice(0, PASSES), nc.scalar.copy)
-            copy_planes(q, 0, slice(0, 1), nc.vector.tensor_copy)
+            copy_planes(q, 0, slice(72, P), nc.scalar.copy)
+            copy_planes(q, 1, slice(0, P), nc.scalar.copy)
+            copy_planes(q, 0, slice(0, 72), nc.vector.tensor_copy)
 
         def quantise(q, tiles=range(PAIR)):
             if 0 in tiles:
@@ -180,7 +180,10 @@ def tile_minerva_old_pa_kernel(tc, features, ex_features, g_weight, out_0, out_1
 
         def multiply(i, h):
             q, a = divmod(i, PAIR)
-            y[i, h] = psum_y.tile([P, N_TILE], F32, name="acc")
+            if i == n_tiles - 3:
+                y[i, h] = psum_t.tile([P, N_TILE], F32, name="acc_t", tag="bank")
+            else:
+                y[i, h] = psum_y.tile([P, N_TILE], F32, name="acc")
             for g in range(PASSES):
                 rows = slice(a * TILE_WORDS + g * P, a * TILE_WORDS + (g + 1) * P)
                 cols = slice(g * F_OUT + h * N_TILE, g * F_OUT + (h + 1) * N_TILE)

from contextlib import ExitStack

import concourse.mybir as mybir
from concourse.masks import make_identity

F32 = mybir.dt.float32
BF16 = mybir.dt.bfloat16
U32 = mybir.dt.uint32
U8 = mybir.dt.uint8
FP8X4 = mybir.dt.float8_e4m3fn_x4
ACT = mybir.ActivationFunctionType
ALU = mybir.AluOpType

P = 128
PACK = 4
K = 1024
K_PASS = P * PACK
PASSES = K // K_PASS
F_OUT = 1024
N_TILE = 512
HALVES = F_OUT // N_TILE
W_TILES = F_OUT // P
PAIR = 2
PLANES = K // 2 // P
TILE_WORDS = PASSES * P
X_AHEAD = 8
BY_HALVES = 4
EPS = 1e-12

FLOPS = 2 * (1024 + 4096) * K * F_OUT


def tile_minerva_old_pa_kernel(tc, features, ex_features, g_weight, out_0, out_1):
    nc = tc.nc

    x_pairs = []
    out_pairs = []
    for x, out in ((features, out_0), (ex_features, out_1)):
        x_view = x.rearrange("(q p a) k -> q p a k", p=P, a=PAIR)
        out_view = out.rearrange("(q p a) f -> q p a f", p=P, a=PAIR)
        for q in range(x.shape[0] // (P * PAIR)):
            x_pairs.append(x_view[q])
            out_pairs.append(out_view[q])
    n_pairs = len(x_pairs)
    n_tiles = n_pairs * PAIR
    w_rows = g_weight.rearrange("(j p) k -> j p k", p=P)

    with ExitStack() as ctx:
        ctx.enter_context(tc.manual_schedule())
        const = ctx.enter_context(tc.tile_pool(name="const", bufs=1))
        w_in = ctx.enter_context(tc.tile_pool(name="w_in", bufs=W_TILES))
        w_stage = ctx.enter_context(tc.tile_pool(name="w_stage", bufs=W_TILES))
        x_in = ctx.enter_context(tc.tile_pool(name="x_in", bufs=X_AHEAD))
        parted = ctx.enter_context(tc.tile_pool(name="parted", bufs=3))
        stage = ctx.enter_context(tc.tile_pool(name="stage", bufs=3))
        small = ctx.enter_context(tc.tile_pool(name="small", bufs=4))
        result = ctx.enter_context(tc.tile_pool(name="result", bufs=10))
        psum_t = ctx.enter_context(tc.psum_pool(name="psum_t", bufs=2))
        psum_y = ctx.enter_context(tc.psum_pool(name="psum_y", bufs=6))

        ident = const.tile([P, P], F32, name="ident")
        make_identity(nc, ident[:])
        warm = const.tile([P, 1], F32, name="warm")
        nc.vector.memset(warm[:], 1.0)
        nc.scalar.activation(out=warm[:], in_=warm[:], func=ACT.Abs_reciprocal_sqrt)

        zeros = const.tile([P, N_TILE], BF16, name="zeros")
        nc.vector.memset(zeros[:], 0.0)
        w_codes = const.tile([P, PASSES * F_OUT], U32, name="w_codes", align_bytes=64)
        w_scales = const.tile([P, PASSES * F_OUT], U8, name="w_scales", align_bytes=64)

        w_raw = {}
        w_grouped = {}
        x_raw = {}
        even_odd = {}
        banks = {}
        grouped = {}
        codes = {}
        scales = {}
        y = {}
        sumsq = {}
        clamped = {}
        rnorm = {}
        unit = {}

        def load_w(j):
            w_raw[j] = w_in.tile([P, K], BF16, name="w_raw")
            nc.sync.dma_start(out=w_raw[j][:], in_=w_rows[j])

        def load_first_pair(a):
            if a == 0:
                x_raw[0] = x_in.tile([P, PAIR, K], BF16, name="x_raw")
            nc.sync.dma_start(out=x_raw[0][:, a, :], in_=x_pairs[0][:, a, :])

        def load_pair(q):
            x_raw[q] = x_in.tile([P, PAIR, K], BF16, name="x_raw")
            nc.sync.dma_start(out=x_raw[q][:], in_=x_pairs[q])

        def transpose_words(rows, bank, parted_words=None):
            words = rows.bitcast(F32)
            for g in range(PASSES):
                for u in range(2):
                    every_2nd = words[:, 2 * P * g + u : 2 * P * (g + 1) : 2]
                    if parted_words is not None:
                        every_2nd = parted_words[:, g, u, :].bitcast(F32)
                    nc.tensor.transpose(bank[:, 2 * g + u, :], every_2nd, ident[:])

        def part_even_odd(q, a):
            even_odd[q, a] = parted.tile([P, PASSES, 2, 2 * P], BF16, name="even_odd", align_bytes=64)
            for g in range(PASSES):
                nc.gpsimd.tensor_scalar(
                    out=even_odd[q, a][:, g].rearrange("p u (w e) -> p u w e", e=2),
                    in0=x_raw[q][:, a, g * K_PASS : (g + 1) * K_PASS].rearrange("p (w u e) -> p u w e", u=2, e=2),
                    scalar1=1.0,
                    scalar2=0.0,
                    op0=ALU.mult,
                    op1=ALU.add,
                )

        def by_row(bank):
            return bank[:].rearrange("p (g u) r -> p g r u", u=2)

        def keep_clock(n):
            idle = psum_y.tile([P, N_TILE], F32, name="idle", tag="acc")
            for c in range(n):
                nc.tensor.matmul(out=idle[:], lhsT=zeros[:, 0:P], rhs=zeros[:], start=True, stop=True)

        def transpose_weights(j):
            banks[j, "w"] = psum_y.tile([P, PLANES, P], F32, name="w_bank", tag="acc")
            transpose_words(w_raw[j][:], banks[j, "w"])

        def regroup_weights(j):
            w_grouped[j] = w_stage.tile([P, TILE_WORDS * PACK], BF16, name="w_grouped", align_bytes=64)
            dest = w_grouped[j][:].bitcast(F32).rearrange("p (g r u) -> p g r u", g=PASSES, u=2)
            if j % 3 != 0:
                nc.scalar.copy(out=dest, in_=by_row(banks[j, "w"]))
            else:
                nc.vector.tensor_copy(out=dest, in_=by_row(banks[j, "w"]))

        def quantise_weights(j):
            for g in range(PASSES):
                cols = slice(g * F_OUT + j * P, g * F_OUT + (j + 1) * P)
                nc.vector.quantize_mx(
                    out=w_codes[:, cols].bitcast(FP8X4),
                    scales=w_scales[:, cols],
                    in_=w_grouped[j][:, g * P * PACK : (g + 1) * P * PACK],
                )

        def transposes(q, tiles=range(PAIR)):
            for a in tiles:
                banks[q, a] = psum_t.tile([P, PLANES, P], F32, name="bank")
                transpose_words(x_raw[q][:, a, :], banks[q, a], even_odd.get((q, a)))

        def copy_planes(q, a, rows, copy):
            dest = grouped[q][:].bitcast(F32).rearrange("p (a g r u) -> p a g r u", a=PAIR, g=PASSES, u=2)
            copy(out=dest[:, a, :, rows], in_=by_row(banks[q, a])[:, :, rows])

        def regroup(q, on_vector, tiles=range(PAIR)):
            if q not in grouped:
                grouped[q] = stage.tile([P, PAIR * TILE_WORDS * PACK], BF16, name="grouped", align_bytes=64)
            for a in tiles:
                copy_planes(q, a, slice(0, P), nc.vector.tensor_copy if a in on_vector else nc.scalar.copy)

        def regroup_shared(q):
            regroup(q, (), ())
            copy_planes(q, 0, slice(72, P), nc.scalar.copy)
            copy_planes(q, 1, slice(0, P), nc.scalar.copy)
            copy_planes(q, 0, slice(0, 72), nc.vector.tensor_copy)

        def quantise(q, tiles=range(PAIR)):
            if 0 in tiles:
                codes[q] = stage.tile([P, PAIR * TILE_WORDS], U32, name="codes", align_bytes=64)
                scales[q] = stage.tile([P, PAIR * TILE_WORDS], U8, name="scales", align_bytes=64)
            words = slice(tiles[0] * TILE_WORDS, (tiles[-1] + 1) * TILE_WORDS)
            nc.vector.quantize_mx(
                out=codes[q][:, words].bitcast(FP8X4),
                scales=scales[q][:, words],
                in_=grouped[q][:, words.start * PACK : words.stop * PACK],
            )

        def multiply(i, h):
            q, a = divmod(i, PAIR)
            if i == n_tiles - 3:
                y[i, h] = psum_t.tile([P, N_TILE], F32, name="acc_t", tag="bank")
            else:
                y[i, h] = psum_y.tile([P, N_TILE], F32, name="acc")
            for g in range(PASSES):
                rows = slice(a * TILE_WORDS + g * P, a * TILE_WORDS + (g + 1) * P)
                cols = slice(g * F_OUT + h * N_TILE, g * F_OUT + (h + 1) * N_TILE)
                nc.tensor.matmul_mx(
                    out=y[i, h][:],
                    lhsT=codes[q][:, rows].bitcast(FP8X4),
                    lhsT_scale=scales[q][:, rows],
                    rhs=w_codes[:, cols].bitcast(FP8X4),
                    rhs_scale=w_scales[:, cols],
                    start=(g == 0),
                    stop=(g == PASSES - 1),
                )

        def square(i, h):
            if h == 0:
                sumsq[i] = small.tile([P, HALVES], F32, name="sumsq")
            squares = stage.tile([P, N_TILE], F32, name="squares")
            nc.scalar.activation(
                out=squares[:], in_=y[i, h][:], func=ACT.Square, accum_out=sumsq[i][:, h : h + 1]
            )

        def clamp(i, engine):
            clamped[i] = small.tile([P, 1], F32, name="clamped")
            engine.tensor_scalar(
                out=clamped[i][:],
                in0=sumsq[i][:, 0:1],
                scalar1=sumsq[i][:, 1:2],
                scalar2=EPS * EPS,
                op0=ALU.add,
                op1=ALU.max,
            )

        def inverse_root(i):
            rnorm[i] = small.tile([P, 1], F32, name="rnorm")
            nc.scalar.activation(out=rnorm[i][:], in_=clamped[i][:], func=ACT.Abs_reciprocal_sqrt)
            unit[i] = result.tile([P, F_OUT], F32, name="unit")

        def scale(i, h):
            nc.vector.tensor_scalar(
                out=unit[i][:, h * N_TILE : (h + 1) * N_TILE],
                in0=y[i, h][:],
                scalar1=rnorm[i][:, 0:1],
                scalar2=None,
                op0=ALU.mult,
            )

        def scale_on_scalar(i, h):
            nc.scalar.activation(
                out=unit[i][:, h * N_TILE : (h + 1) * N_TILE],
                in_=y[i, h][:],
                func=ACT.Copy,
                scale=rnorm[i][:, 0:1],
            )

        def store(i):
            q, a = divmod(i, PAIR)
            nc.sync.dma_start(out=out_pairs[q][:, a, :], in_=unit[i][:])

        def store_half(i, h, engine):
            q, a = divmod(i, PAIR)
            cols = slice(h * N_TILE, (h + 1) * N_TILE)
            engine.dma_start(out=out_pairs[q][:, a, cols], in_=unit[i][:, cols])

        for j in range(W_TILES // HALVES):
            load_w(j)
        load_first_pair(0)
        for j in range(W_TILES // HALVES, W_TILES):
            load_w(j)
        load_first_pair(1)
        for q in range(1, X_AHEAD):
            load_pair(q)

        first, second = (0,), (1,)
        keep_clock(5)
        for j in range(W_TILES):
            if j in (2, 4, 6):
                keep_clock(1)
            if j == W_TILES // HALVES:
                transposes(0, first)
                regroup(0, (), first)
            transpose_weights(j)
            regroup_weights(j)
            if j >= 1:
                quantise_weights(j - 1)
            if j == W_TILES // HALVES:
                quantise(0, first)
        transposes(0, second)
        regroup(0, (), second)
        multiply(0, 0)
        square(0, 0)
        quantise_weights(W_TILES - 1)
        quantise(0, second)
        transposes(1)
        regroup(1, on_vector=(0, 1))
        multiply(0, 1)
        square(0, 1)
        quantise(1)
        clamp(0, nc.vector)
        multiply(1, 0)
        square(1, 0)
        inverse_root(0)
        multiply(1, 1)
        square(1, 1)
        scale(0, 0)
        clamp(1, nc.vector)
        scale(0, 1)
        store(0)

        for i in range(n_tiles):
            q, a = divmod(i, PAIR)
            if q >= 1:
                multiply(i, 0)
                multiply(i, 1)
                square(i, 0)
                inverse_root(i - 1)
                square(i, 1)
            if a == 0:
                if q + X_AHEAD < n_pairs:
                    load_pair(q + X_AHEAD)
                if q + 2 < n_pairs:
                    transposes(q + 2)
                if 1 <= q < n_pairs - 1:
                    quantise(q + 1)
            if a == 1 and q + 3 < n_pairs:
                for b in (0,):
                    part_even_odd(q + 3, b)
            if 2 <= i < n_tiles - 1:
                scale(i - 1, 0)
                if i - 1 >= n_tiles - BY_HALVES:
                    store_half(i - 1, 0, nc.sync)
                if q >= 1:
                    clamp(i, nc.vector)
                scale(i - 1, 1)
                if i - 1 < n_tiles - BY_HALVES:
                    store(i - 1)
                else:
                    store_half(i - 1, 1, nc.sync)
            if a == 0 and q + 2 < n_pairs:
                regroup_shared(q + 2)

        last = n_tiles - 1
        scale(last - 1, 1)
        store_half(last - 1, 1, nc.sync)
        scale_on_scalar(last - 1, 0)
        store_half(last - 1, 0, nc.sync)
        clamp(last, nc.vector)
        inverse_root(last)
        scale_on_scalar(last, 0)
        store_half(last, 0, nc.scalar)
        scale(last, 1)
        store_half(last, 1, nc.sync)
